import numpy as np
import ml_dtypes


def mxq(x, axis, fmt="e4m3"):
    dtype, down = {"e4m3": (ml_dtypes.float8_e4m3fn, 7), "e5m2": (ml_dtypes.float8_e5m2, 14)}[fmt]
    v = np.moveaxis(np.asarray(x, np.float32).astype(ml_dtypes.bfloat16).astype(np.float64), axis, -1)
    blocks = v.reshape(v.shape[:-1] + (-1, 32))
    amax = np.abs(blocks).max(-1, keepdims=True)
    byte = np.maximum(np.where(amax > 0, np.frexp(amax)[1] - 1 + 127, 0) - down, 1)
    scale = np.exp2(byte - 127.0)
    codes = (blocks / scale).astype(np.float32).astype(dtype).astype(np.float64)
    return np.moveaxis((codes * scale).reshape(v.shape), -1, axis)


WIDE = False


def mx_kscale(k):
    if not WIDE:
        return np.ones(k)
    levels = np.array([10, -10, 5, -5, 0])
    if k % 512:
        return np.exp2(np.random.permutation(np.resize(levels, k // 32))).repeat(32)
    a = np.empty((k // 512, 16))
    for p in range(k // 512):
        a[p, :8] = np.random.permutation(np.resize(levels, 8))
        for g in range(8):
            far = levels[np.abs(levels - a[p, g]) >= 10]
            a[p, g + 8] = far[np.random.randint(len(far))]
    return np.exp2(a.ravel()).repeat(32)


BF16 = ml_dtypes.bfloat16


def bf(x):
    return np.asarray(x, np.float32).astype(BF16)


def f64(x):
    return np.asarray(x).astype(np.float64)


B, L, E, H, DH, RK, RD, MAXLEN = 4, 128, 2048, 16, 128, 512, 128, 4096


def apply_rope(x, cos, sin):
    cos = cos[None, :, None, :]
    sin = sin[None, :, None, :]
    x1, x2 = x[..., 0::2], x[..., 1::2]
    out_real = x1 * cos - x2 * sin
    out_imag = x1 * sin + x2 * cos
    return np.stack([out_real, out_imag], axis=-1).reshape(x.shape)


def draw0():
    s = mx_kscale(E)
    return {"x": bf(np.random.standard_normal((B, L, E)) * s),
            "cos": bf(np.random.uniform(size=(L, RD // 2))),
            "sin": bf(np.random.uniform(size=(L, RD // 2))),
            "wq": bf(np.random.standard_normal((E, H * (DH + RD))) / np.sqrt(E) / s[:, None])}


def core(x, cos, sin, wq):
    q_all = (mxq(f64(x), 2, "e4m3") @ mxq(f64(wq), 0, "e4m3")).reshape(B, L, H, DH + RD)
    q_head, q_rope = q_all[..., :DH], q_all[..., DH:]
    q_rope = apply_rope(q_rope, f64(cos), f64(sin))
    return np.concatenate([q_head, q_rope], axis=-1)


def e4m3fn_bytes(y):
    return np.clip(np.asarray(y, np.float64), -448.0, 448.0).astype(np.float32).astype(ml_dtypes.float8_e4m3fn).view(np.uint8)


def e4m3fn_values(b):
    return np.asarray(b, np.uint8).view(ml_dtypes.float8_e4m3fn).astype(np.float64)


def setup_inputs():
    d = draw0()
    x0 = np.asarray(d['wq']).astype(np.float64)
    s = (np.max(np.abs(x0), axis=(1,), keepdims=True) / 448.0).astype(np.float32)
    out = {}
    for k, v in d.items():
        if k == 'wq':
            out['wq_bytes'] = e4m3fn_bytes(x0 / s.astype(np.float64))
            out['wq_scale'] = s
        else:
            out[k] = v
    return out


def reference(x, cos, sin, wq_bytes, wq_scale):
    return core(x, cos, sin, e4m3fn_values(wq_bytes) * wq_scale.astype(np.float64))

@@ -1,0 +1,296 @@
+from contextlib import ExitStack
+
+import concourse.mybir as mybir
+from concourse.masks import make_identity
+
+F32 = mybir.dt.float32
+BF16 = mybir.dt.bfloat16
+U32 = mybir.dt.uint32
+U8 = mybir.dt.uint8
+FP8 = mybir.dt.float8_e4m3fn
+FP8X4 = mybir.dt.float8_e4m3fn_x4
+MULT = mybir.AluOpType.mult
+ADD = mybir.AluOpType.add
+COPY = mybir.ActivationFunctionType.Copy
+
+P = 128
+PACK = 4
+PASSES = 4
+TOK = 4
+E = 2048
+LOAD_COLS = 1024
+LOADS = 16
+BANK = 512
+LEAD = 2
+CHUNK_HEADS = (4, 4, 4, 2, 2)
+CHUNKS = 5
+UNITS = 20
+
+FLOPS = 2 * 512 * 2048 * 4096
+
+PE_COLS = (512, 256, 512, 256, 512, 256, 512, 256, 512, 256, 512, 256, 256, 0, 256, 0, 256, 0, 256, 256)
+V_PLANES = (3, 4, 2, 1, 1, 1, 1, 0, 1, 1, 1, 0, 1, 0, 0, 0, 0, 0, 0, 0)
+S_COLS = (256, 128, 0, 0, 0, 0, 0, 0, 0, 0, 0, 0, 0, 0, 0, 0, 0, 0, 0, 0)
+FAST_IL = False
+
+
+def tile_multiheadlatentattention_pb_kernel(tc, x, cos, sin, wq_bytes, wq_scale, out):
+    nc = tc.nc
+    w_view = wq_bytes.rearrange("(g p t) n -> g p t n", p=P, t=PACK)
+    s_view = wq_scale.rearrange("(g p t) o -> p g (t o)", p=P, t=PACK)
+    out_view = out.rearrange("b l h (q d) -> b q l h d", q=2)
+
+    with ExitStack() as ctx:
+        const = ctx.enter_context(tc.tile_pool(name="const", bufs=1))
+        wpool = ctx.enter_context(tc.tile_pool(name="wpool", bufs=LOADS))
+        xpool = ctx.enter_context(tc.tile_pool(name="xpool", bufs=2))
+        stage = ctx.enter_context(tc.tile_pool(name="stage", bufs=2))
+        codes = ctx.enter_context(tc.tile_pool(name="codes", bufs=8))
+        outs = ctx.enter_context(tc.tile_pool(name="outs", bufs=3))
+        psum = ctx.enter_context(tc.psum_pool(name="psum", bufs=2))
+        ctx.enter_context(tc.manual_schedule())
+
+        wsc = const.tile([P, PASSES, PACK], F32, name="wsc")
+        cos_sb = const.tile([P, 64], BF16, name="cos_sb")
+        sin_sb = const.tile([P, 64], BF16, name="sin_sb")
+        cc4 = const.tile([P, BANK], F32, name="cc4")
+        ss4 = const.tile([P, BANK], F32, name="ss4")
+        ident = const.tile([P, P], F32, name="ident")
+        ident_bf = const.tile([P, P], BF16, name="ident_bf")
+
+        wb = {}
+        x_sb = {}
+        xt = {}
+        xg = {}
+        xc = {}
+        xs = {}
+        pl = {}
+        gr = {}
+        wc = {}
+        ws = {}
+        acc = {}
+        rp = {}
+        tm = {}
+
+        def load_w(i):
+            c, g = divmod(i, PASSES)
+            wb[i] = wpool.tile([P, PACK, LOAD_COLS], U8, name="wb")
+            if i == 0:
+                for t in range(PACK):
+                    nc.sync.dma_start(out=wb[i][:, t, :], in_=w_view[g][:, t, :LOAD_COLS])
+            else:
+                nc.sync.dma_start(out=wb[i][:], in_=w_view[g][:, :, c * LOAD_COLS:(c + 1) * LOAD_COLS])
+
+        def cols(u):
+            c = u // PASSES
+            return 256 * sum(CHUNK_HEADS[:c]), 256 * CHUNK_HEADS[c]
+
+        def load_x(m):
+            x_sb[m] = xpool.tile([P, E], BF16, name="x_sb", bufs=TOK)
+            nc.sync.dma_start(out=x_sb[m][:], in_=x[m])
+
+        def x_transposes(m):
+            words = x_sb[m][:].bitcast(F32)
+            for half in range(2):
+                xt[(m, half)] = psum.tile([P, 4, P], F32, name="acc%d" % half, bufs=2 + half)
+                for gu in range(4):
+                    g = 2 * half + gu // 2
+                    u = gu % 2
+                    nc.tensor.transpose(xt[(m, half)][:, gu, :], words[:, 256 * g + u:256 * (g + 1):2], ident[:])
+
+        def x_evac(m, half):
+            if m % 2 == 0 and half == 0:
+                xg[m // 2] = xpool.tile([P, 2, PASSES * P * PACK], BF16, name="xg", align_bytes=64)
+            dst = xg[m // 2][:, m % 2, :].bitcast(F32).rearrange("p (g r u) -> p g r u", g=PASSES, u=2)[:, 2 * half:2 * half + 2]
+            nc.vector.tensor_copy(out=dst, in_=xt[(m, half)][:].rearrange("p (g u) r -> p g r u", u=2))
+
+        def x_quant(mm):
+            xc[mm] = xpool.tile([P, 2 * PASSES * P], U32, name="xc", align_bytes=64)
+            xs[mm] = xpool.tile([P, 2 * PASSES * P], U8, name="xs", align_bytes=64)
+            nc.vector.quantize_mx(out=xc[mm][:].bitcast(FP8X4), scales=xs[mm][:], in_=xg[mm][:].rearrange("p a c -> p (a c)"))
+
+        def widen(u, on_vector, planes):
+            if not 0 <= u < UNITS:
+                return
+            g = u % PASSES
+            c0, n = cols(u)
+            i = (c0 // LOAD_COLS) * PASSES + g
+            o = c0 % LOAD_COLS
+            if on_vector:
+                pl[u] = stage.tile([P, PACK, n], BF16, name="pl", bufs=4)
+            elif 0 in planes:
+                gr[u] = stage.tile([P, n * PACK], BF16, name="gr", bufs=3, align_bytes=64)
+            for t in planes:
+                src = wb[i][:, t, o:o + n].bitcast(FP8)
+                if t < V_PLANES[u] and on_vector:
+                    nc.vector.tensor_scalar(out=pl[u][:, t, :], in0=src, scalar1=wsc[:, g, t:t + 1], scalar2=None, op0=MULT)
+                if t >= V_PLANES[u] and not on_vector:
+                    nc.scalar.activation(out=pl[u][:, t, :], in_=src, func=COPY, scale=wsc[:, g, t:t + 1])
+
+        def il_views(u, n0, n1):
+            if FAST_IL:
+                return (gr[u][:, PACK * n0:PACK * n1].rearrange("p (c i t) -> p c t i", i=4, t=PACK),
+                        pl[u][:, :, n0:n1].rearrange("p t (c i) -> p c t i", i=4))
+            return (gr[u][:, PACK * n0:PACK * n1].rearrange("p (n t) -> p n t", t=PACK),
+                    pl[u][:, :, n0:n1].rearrange("p t n -> p n t"))
+
+        def interleave_s(u):
+            n = cols(u)[1]
+            if S_COLS[u] > 0:
+                dst, src = il_views(u, n - PE_COLS[u] - S_COLS[u], n - PE_COLS[u])
+                nc.scalar.copy(out=dst, in_=src)
+
+        def interleave_v(u):
+            n = cols(u)[1]
+            dst, src = il_views(u, 0, n - PE_COLS[u] - S_COLS[u])
+            nc.vector.tensor_copy(out=dst, in_=src)
+
+        def interleave_pe(u):
+            n = cols(u)[1]
+            for b0 in range(n - PE_COLS[u], n, 256):
+                il = psum.tile([P, 1024], BF16, name="il", bufs=3)
+                for j in range(2):
+                    n0 = b0 + 128 * j
+                    nc.tensor.matmul(out=il[:, 512 * j:512 * (j + 1)].rearrange("p (n t) -> p n t", t=PACK),
+                                     lhsT=ident_bf[:], rhs=pl[u][:, :, n0:n0 + 128].rearrange("p t n -> p n t"),
+                                     start=True, stop=True)
+                nc.scalar.copy(out=gr[u][:, PACK * b0:PACK * b0 + 1024], in_=il[:])
+
+        def quant(u):
+            n = cols(u)[1]
+            wc[u] = codes.tile([P, n], U32, name="wc", align_bytes=64)
+            ws[u] = codes.tile([P, n], U8, name="ws", align_bytes=64)
+            nc.vector.quantize_mx(out=wc[u][:].bitcast(FP8X4), scales=ws[u][:], in_=gr[u][:])
+
+        def task_tiles(c, j):
+            per = TOK // CHUNK_HEADS[c]
+            return range(j * per, (j + 1) * per)
+
+        def group(c, j, q):
+            hc = CHUNK_HEADS[c]
+            acc[(c, j, q)] = psum.tile([P, BANK], F32, name="acc%d" % q, bufs=2 + q)
+            for a, m in enumerate(task_tiles(c, j)):
+                for h in range(hc):
+                    n0 = 256 * h + 128 * q
+                    o = 128 * (a * hc + h)
+                    for g in range(PASSES):
+                        u = c * PASSES + g
+                        k0 = (m % 2) * PASSES * P + P * g
+                        nc.tensor.matmul_mx(
+                            out=acc[(c, j, q)][:, o:o + 128],
+                            lhsT=xc[m // 2][:, k0:k0 + P].bitcast(FP8X4),
+                            lhsT_scale=xs[m // 2][:, k0:k0 + P],
+                            rhs=wc[u][:, n0:n0 + 128].bitcast(FP8X4),
+                            rhs_scale=ws[u][:, n0:n0 + 128],
+                            start=(g == 0), stop=(g == PASSES - 1))
+
+        def store(c, j, q, tile):
+            hc = CHUNK_HEADS[c]
+            h0 = sum(CHUNK_HEADS[:c])
+            for a, m in enumerate(task_tiles(c, j)):
+                nc.sync.dma_start(out=out_view[m][q][:, h0:h0 + hc, :],
+                                  in_=tile[:, 128 * hc * a:128 * hc * (a + 1)].rearrange("p (h d) -> p h d", d=128))
+
+        def content(c, j):
+            oc = outs.tile([P, BANK], F32, name="oc", bufs=3)
+            nc.scalar.copy(out=oc[:], in_=acc[(c, j, 0)][:])
+            store(c, j, 0, oc)
+
+        def rope_products(c, j):
+            r = acc[(c, j, 1)]
+            rp[(c, j)] = outs.tile([P, BANK], F32, name="rp", bufs=5)
+            tm[(c, j)] = outs.tile([P, BANK], F32, name="tm", bufs=3)
+            nc.vector.tensor_tensor(out=rp[(c, j)][:], in0=r[:], in1=cc4[:], op=MULT)
+            nc.vector.tensor_tensor(out=tm[(c, j)][:].rearrange("p (j e) -> p j e", e=2),
+                                    in0=r[:].rearrange("p (j e) -> p j e", e=2)[:, :, ::-1],
+                                    in1=ss4[:].rearrange("p (j e) -> p j e", e=2), op=MULT)
+
+        def rope_sum(c, j, eng):
+            eng.tensor_tensor(out=rp[(c, j)][:], in0=rp[(c, j)][:], in1=tm[(c, j)][:], op=ADD)
+            store(c, j, 1, rp[(c, j)])
+
+        nc.scalar.dma_start(out=wsc[:], in_=s_view)
+        nc.scalar.dma_start(out=cos_sb[:], in_=cos)
+        nc.scalar.dma_start(out=sin_sb[:], in_=sin)
+        for i in range(3):
+            load_w(i)
+        load_x(0)
+        load_x(1)
+        load_w(3)
+        load_x(2)
+        load_x(3)
+        for i in range(4, LOADS):
+            load_w(i)
+        make_identity(nc, ident[:])
+        make_identity(nc, ident_bf[:])
+
+        bshape = [P, 4, 64, 2]
+        nc.scalar.copy(out=cc4[:].rearrange("p (h j e) -> p h j e", h=4, e=2),
+                       in_=cos_sb[:].unsqueeze(1).unsqueeze(3).to_broadcast(bshape))
+        sin_b = sin_sb[:].unsqueeze(1).to_broadcast([P, 4, 64])
+        ss_v = ss4[:].rearrange("p (h j e) -> p h j e", h=4, e=2)
+        nc.scalar.activation(out=ss_v[:, :, :, 0], in_=sin_b, func=COPY, scale=-1.0)
+        nc.scalar.copy(out=ss_v[:, :, :, 1], in_=sin_b)
+
+        waiting = []
+        filled = []
+        ready = []
+        summed = []
+
+        def rope_ready():
+            for task in ready:
+                rope_products(task[0], task[1])
+            summed.extend(ready)
+            ready.clear()
+
+        s = -LEAD - 1
+        while s < UNITS or waiting or filled or ready or summed:
+            widen(s + LEAD, False, (0, 1, 2))
+            if 0 <= s + 1 < UNITS:
+                interleave_pe(s + 1)
+            if s == -1:
+                x_transposes(0)
+                x_transposes(1)
+            done = list(filled)
+            filled.clear()
+            if s >= UNITS and waiting:
+                for q in (1, 0):
+                    for task in waiting:
+                        group(task[0], task[1], q)
+                filled.extend(waiting)
+                waiting.clear()
+            elif waiting:
+                task = waiting.pop(0)
+                group(task[0], task[1], 1)
+                group(task[0], task[1], 0)
+                filled.append(task)
+            widen(s + LEAD, False, (3,))
+            for task in done:
+                content(task[0], task[1])
+            if 0 <= s + LEAD < UNITS:
+                interleave_s(s + LEAD)
+            if 0 <= s < UNITS:
+                interleave_v(s)
+            if 0 <= s < TOK:
+                x_evac(s, 0)
+                x_evac(s, 1)
+                if s + 2 < TOK:
+                    x_transposes(s + 2)
+            ready.extend(done)
+            hold = UNITS - PASSES < s < UNITS
+            if (ready and not hold) or (ready and not waiting and not filled and s >= UNITS):
+                rope_ready()
+            if 0 <= s < UNITS:
+                quant(s)
+                if s % PASSES == PASSES - 1:
+                    c = s // PASSES
+                    waiting.extend([(c, j) for j in range(CHUNK_HEADS[c])])
+            if s == UNITS - 1 and ready:
+                rope_ready()
+            if s in (1, 3):
+                x_quant(s // 2)
+            widen(s + LEAD + 1, True, (0, 1, 2, 3))
+            for task in summed:
+                rope_sum(task[0], task[1], nc.vector)
+            summed.clear()
+            s += 1

@@ -31,7 +31,6 @@ FLOPS = 2 * 512 * 2048 * 4096
 PE_COLS = (512, 256, 512, 256, 512, 256, 512, 256, 512, 256, 512, 256, 256, 0, 256, 0, 256, 0, 256, 256)
 V_PLANES = (3, 4, 2, 1, 1, 1, 1, 0, 1, 1, 1, 0, 1, 0, 0, 0, 0, 0, 0, 0)
 S_COLS = (256, 128, 0, 0, 0, 0, 0, 0, 0, 0, 0, 0, 0, 0, 0, 0, 0, 0, 0, 0)
-FAST_IL = False
 
 
 def tile_multiheadlatentattention_pb_kernel(tc, x, cos, sin, wq_bytes, wq_scale, out):
@@ -127,30 +126,36 @@ def tile_multiheadlatentattention_pb_kernel(tc, x, cos, sin, wq_bytes, wq_scale,
                 if t >= V_PLANES[u] and not on_vector:
                     nc.scalar.activation(out=pl[u][:, t, :], in_=src, func=COPY, scale=wsc[:, g, t:t + 1])
 
-        def il_views(u, n0, n1):
-            if FAST_IL:
-                return (gr[u][:, PACK * n0:PACK * n1].rearrange("p (c i t) -> p c t i", i=4, t=PACK),
-                        pl[u][:, :, n0:n1].rearrange("p t (c i) -> p c t i", i=4))
-            return (gr[u][:, PACK * n0:PACK * n1].rearrange("p (n t) -> p n t", t=PACK),
-                    pl[u][:, :, n0:n1].rearrange("p t n -> p n t"))
+        def il_copies(u, n0, n1):
+            half = cols(u)[1] // 2
+            views = []
+            for q in range(2):
+                a = max(n0, q * half)
+                b = min(n1, (q + 1) * half)
+                if a < b:
+                    views.append((gr[u][:, PACK * a:PACK * b].rearrange("p (h d t) -> p h d t", d=128, t=PACK),
+                                  pl[u][:].rearrange("p t (h q d) -> p q h d t", q=2, d=128)[:, q, (a - q * half) // 128:(b - q * half) // 128]))
+            return views
 
         def interleave_s(u):
             n = cols(u)[1]
             if S_COLS[u] > 0:
-                dst, src = il_views(u, n - PE_COLS[u] - S_COLS[u], n - PE_COLS[u])
-                nc.scalar.copy(out=dst, in_=src)
+                for dst, src in il_copies(u, n - PE_COLS[u] - S_COLS[u], n - PE_COLS[u]):
+                    nc.scalar.copy(out=dst, in_=src)
 
         def interleave_v(u):
             n = cols(u)[1]
-            dst, src = il_views(u, 0, n - PE_COLS[u] - S_COLS[u])
-            nc.vector.tensor_copy(out=dst, in_=src)
+            for dst, src in il_copies(u, 0, n - PE_COLS[u] - S_COLS[u]):
+                nc.vector.tensor_copy(out=dst, in_=src)
 
         def interleave_pe(u):
             n = cols(u)[1]
+            hc = n // 256
             for b0 in range(n - PE_COLS[u], n, 256):
                 il = psum.tile([P, 1024], BF16, name="il", bufs=3)
                 for j in range(2):
-                    n0 = b0 + 128 * j
+                    q, h = divmod(b0 // 128 + j, hc)
+                    n0 = 256 * h + 128 * q
                     nc.tensor.matmul(out=il[:, 512 * j:512 * (j + 1)].rearrange("p (n t) -> p n t", t=PACK),
                                      lhsT=ident_bf[:], rhs=pl[u][:, :, n0:n0 + 128].rearrange("p t n -> p n t"),
                                      start=True, stop=True)
@@ -169,20 +174,18 @@ def tile_multiheadlatentattention_pb_kernel(tc, x, cos, sin, wq_bytes, wq_scale,
         def group(c, j, q):
             hc = CHUNK_HEADS[c]
             acc[(c, j, q)] = psum.tile([P, BANK], F32, name="acc%d" % q, bufs=2 + q)
+            w = 128 * hc
             for a, m in enumerate(task_tiles(c, j)):
-                for h in range(hc):
-                    n0 = 256 * h + 128 * q
-                    o = 128 * (a * hc + h)
-                    for g in range(PASSES):
-                        u = c * PASSES + g
-                        k0 = (m % 2) * PASSES * P + P * g
-                        nc.tensor.matmul_mx(
-                            out=acc[(c, j, q)][:, o:o + 128],
-                            lhsT=xc[m // 2][:, k0:k0 + P].bitcast(FP8X4),
-                            lhsT_scale=xs[m // 2][:, k0:k0 + P],
-                            rhs=wc[u][:, n0:n0 + 128].bitcast(FP8X4),
-                            rhs_scale=ws[u][:, n0:n0 + 128],
-                            start=(g == 0), stop=(g == PASSES - 1))
+                for g in range(PASSES):
+                    u = c * PASSES + g
+                    k0 = (m % 2) * PASSES * P + P * g
+                    nc.tensor.matmul_mx(
+                        out=acc[(c, j, q)][:, w * a:w * (a + 1)],
+                        lhsT=xc[m // 2][:, k0:k0 + P].bitcast(FP8X4),
+                        lhsT_scale=xs[m // 2][:, k0:k0 + P],
+                        rhs=wc[u][:, w * q:w * (q + 1)].bitcast(FP8X4),
+                        rhs_scale=ws[u][:, w * q:w * (q + 1)],
+                        start=(g == 0), stop=(g == PASSES - 1))
 
         def store(c, j, q, tile):
             hc = CHUNK_HEADS[c]

@@ -133,8 +133,8 @@ def tile_multiheadlatentattention_pb_kernel(tc, x, cos, sin, wq_bytes, wq_scale,
                 a = max(n0, q * half)
                 b = min(n1, (q + 1) * half)
                 if a < b:
-                    views.append((gr[u][:, PACK * a:PACK * b].rearrange("p (h d t) -> p h d t", d=128, t=PACK),
-                                  pl[u][:].rearrange("p t (h q d) -> p q h d t", q=2, d=128)[:, q, (a - q * half) // 128:(b - q * half) // 128]))
+                    views.append((gr[u][:, PACK * a:PACK * b].rearrange("p (h c i t) -> p h c t i", c=32, i=4, t=PACK),
+                                  pl[u][:].rearrange("p t (h q c i) -> p q h c t i", q=2, c=32, i=4)[:, q, (a - q * half) // 128:(b - q * half) // 128]))
             return views
 
         def interleave_s(u):

from contextlib import ExitStack

import concourse.mybir as mybir
from concourse.masks import make_identity

F32 = mybir.dt.float32
BF16 = mybir.dt.bfloat16
U32 = mybir.dt.uint32
U8 = mybir.dt.uint8
FP8 = mybir.dt.float8_e4m3fn
FP8X4 = mybir.dt.float8_e4m3fn_x4
MULT = mybir.AluOpType.mult
ADD = mybir.AluOpType.add
COPY = mybir.ActivationFunctionType.Copy

P = 128
PACK = 4
PASSES = 4
TOK = 4
E = 2048
LOAD_COLS = 1024
LOADS = 16
BANK = 512
LEAD = 2
CHUNK_HEADS = (4, 4, 4, 2, 2)
CHUNKS = 5
UNITS = 20

FLOPS = 2 * 512 * 2048 * 4096

PE_COLS = (512, 256, 512, 256, 512, 256, 512, 256, 512, 256, 512, 256, 256, 0, 256, 0, 256, 0, 256, 256)
V_PLANES = (3, 4, 2, 1, 1, 1, 1, 0, 1, 1, 1, 0, 1, 0, 0, 0, 0, 0, 0, 0)
S_COLS = (256, 128, 0, 0, 0, 0, 0, 0, 0, 0, 0, 0, 0, 0, 0, 0, 0, 0, 0, 0)


def tile_multiheadlatentattention_pb_kernel(tc, x, cos, sin, wq_bytes, wq_scale, out):
    nc = tc.nc
    w_view = wq_bytes.rearrange("(g p t) n -> g p t n", p=P, t=PACK)
    s_view = wq_scale.rearrange("(g p t) o -> p g (t o)", p=P, t=PACK)
    out_view = out.rearrange("b l h (q d) -> b q l h d", q=2)

    with ExitStack() as ctx:
        const = ctx.enter_context(tc.tile_pool(name="const", bufs=1))
        wpool = ctx.enter_context(tc.tile_pool(name="wpool", bufs=LOADS))
        xpool = ctx.enter_context(tc.tile_pool(name="xpool", bufs=2))
        stage = ctx.enter_context(tc.tile_pool(name="stage", bufs=2))
        codes = ctx.enter_context(tc.tile_pool(name="codes", bufs=8))
        outs = ctx.enter_context(tc.tile_pool(name="outs", bufs=3))
        psum = ctx.enter_context(tc.psum_pool(name="psum", bufs=2))
        ctx.enter_context(tc.manual_schedule())

        wsc = const.tile([P, PASSES, PACK], F32, name="wsc")
        cos_sb = const.tile([P, 64], BF16, name="cos_sb")
        sin_sb = const.tile([P, 64], BF16, name="sin_sb")
        cc4 = const.tile([P, BANK], F32, name="cc4")
        ss4 = const.tile([P, BANK], F32, name="ss4")
        ident = const.tile([P, P], F32, name="ident")
        ident_bf = const.tile([P, P], BF16, name="ident_bf")

        wb = {}
        x_sb = {}
        xt = {}
        xg = {}
        xc = {}
        xs = {}
        pl = {}
        gr = {}
        wc = {}
        ws = {}
        acc = {}
        rp = {}
        tm = {}

        def load_w(i):
            c, g = divmod(i, PASSES)
            wb[i] = wpool.tile([P, PACK, LOAD_COLS], U8, name="wb")
            if i == 0:
                for t in range(PACK):
                    nc.sync.dma_start(out=wb[i][:, t, :], in_=w_view[g][:, t, :LOAD_COLS])
            else:
                nc.sync.dma_start(out=wb[i][:], in_=w_view[g][:, :, c * LOAD_COLS:(c + 1) * LOAD_COLS])

        def cols(u):
            c = u // PASSES
            return 256 * sum(CHUNK_HEADS[:c]), 256 * CHUNK_HEADS[c]

        def load_x(m):
            x_sb[m] = xpool.tile([P, E], BF16, name="x_sb", bufs=TOK)
            nc.sync.dma_start(out=x_sb[m][:], in_=x[m])

        def x_transposes(m):
            words = x_sb[m][:].bitcast(F32)
            for half in range(2):
                xt[(m, half)] = psum.tile([P, 4, P], F32, name="acc%d" % half, bufs=2 + half)
                for gu in range(4):
                    g = 2 * half + gu // 2
                    u = gu % 2
                    nc.tensor.transpose(xt[(m, half)][:, gu, :], words[:, 256 * g + u:256 * (g + 1):2], ident[:])

        def x_evac(m, half):
            if m % 2 == 0 and half == 0:
                xg[m // 2] = xpool.tile([P, 2, PASSES * P * PACK], BF16, name="xg", align_bytes=64)
            dst = xg[m // 2][:, m % 2, :].bitcast(F32).rearrange("p (g r u) -> p g r u", g=PASSES, u=2)[:, 2 * half:2 * half + 2]
            nc.vector.tensor_copy(out=dst, in_=xt[(m, half)][:].rearrange("p (g u) r -> p g r u", u=2))

        def x_quant(mm):
            xc[mm] = xpool.tile([P, 2 * PASSES * P], U32, name="xc", align_bytes=64)
            xs[mm] = xpool.tile([P, 2 * PASSES * P], U8, name="xs", align_bytes=64)
            nc.vector.quantize_mx(out=xc[mm][:].bitcast(FP8X4), scales=xs[mm][:], in_=xg[mm][:].rearrange("p a c -> p (a c)"))

        def widen(u, on_vector, planes):
            if not 0 <= u < UNITS:
                return
            g = u % PASSES
            c0, n = cols(u)
            i = (c0 // LOAD_COLS) * PASSES + g
            o = c0 % LOAD_COLS
            if on_vector:
                pl[u] = stage.tile([P, PACK, n], BF16, name="pl", bufs=4)
            elif 0 in planes:
                gr[u] = stage.tile([P, n * PACK], BF16, name="gr", bufs=3, align_bytes=64)
            for t in planes:
                src = wb[i][:, t, o:o + n].bitcast(FP8)
                if t < V_PLANES[u] and on_vector:
                    nc.vector.tensor_scalar(out=pl[u][:, t, :], in0=src, scalar1=wsc[:, g, t:t + 1], scalar2=None, op0=MULT)
                if t >= V_PLANES[u] and not on_vector:
                    nc.scalar.activation(out=pl[u][:, t, :], in_=src, func=COPY, scale=wsc[:, g, t:t + 1])

        def il_copies(u, n0, n1):
            half = cols(u)[1] // 2
            views = []
            for q in range(2):
                a = max(n0, q * half)
                b = min(n1, (q + 1) * half)
                if a < b:
                    views.append((gr[u][:, PACK * a:PACK * b].rearrange("p (h c i t) -> p h c t i", c=32, i=4, t=PACK),
                                  pl[u][:].rearrange("p t (h q c i) -> p q h c t i", q=2, c=32, i=4)[:, q, (a - q * half) // 128:(b - q * half) // 128]))
            return views

        def interleave_s(u):
            n = cols(u)[1]
            if S_COLS[u] > 0:
                for dst, src in il_copies(u, n - PE_COLS[u] - S_COLS[u], n - PE_COLS[u]):
                    nc.scalar.copy(out=dst, in_=src)

        def interleave_v(u):
            n = cols(u)[1]
            for dst, src in il_copies(u, 0, n - PE_COLS[u] - S_COLS[u]):
                nc.vector.tensor_copy(out=dst, in_=src)

        def interleave_pe(u):
            n = cols(u)[1]
            hc = n // 256
            for b0 in range(n - PE_COLS[u], n, 256):
                il = psum.tile([P, 1024], BF16, name="il", bufs=3)
                for j in range(2):
                    q, h = divmod(b0 // 128 + j, hc)
                    n0 = 256 * h + 128 * q
                    nc.tensor.matmul(out=il[:, 512 * j:512 * (j + 1)].rearrange("p (n t) -> p n t", t=PACK),
                                     lhsT=ident_bf[:], rhs=pl[u][:, :, n0:n0 + 128].rearrange("p t n -> p n t"),
                                     start=True, stop=True)
                nc.scalar.copy(out=gr[u][:, PACK * b0:PACK * b0 + 1024], in_=il[:])

        def quant(u):
            n = cols(u)[1]
            wc[u] = codes.tile([P, n], U32, name="wc", align_bytes=64)
            ws[u] = codes.tile([P, n], U8, name="ws", align_bytes=64)
            nc.vector.quantize_mx(out=wc[u][:].bitcast(FP8X4), scales=ws[u][:], in_=gr[u][:])

        def task_tiles(c, j):
            per = TOK // CHUNK_HEADS[c]
            return range(j * per, (j + 1) * per)

        def group(c, j, q):
            hc = CHUNK_HEADS[c]
            acc[(c, j, q)] = psum.tile([P, BANK], F32, name="acc%d" % q, bufs=2 + q)
            w = 128 * hc
            for a, m in enumerate(task_tiles(c, j)):
                for g in range(PASSES):
                    u = c * PASSES + g
                    k0 = (m % 2) * PASSES * P + P * g
                    nc.tensor.matmul_mx(
                        out=acc[(c, j, q)][:, w * a:w * (a + 1)],
                        lhsT=xc[m // 2][:, k0:k0 + P].bitcast(FP8X4),
                        lhsT_scale=xs[m // 2][:, k0:k0 + P],
                        rhs=wc[u][:, w * q:w * (q + 1)].bitcast(FP8X4),
                        rhs_scale=ws[u][:, w * q:w * (q + 1)],
                        start=(g == 0), stop=(g == PASSES - 1))

        def store(c, j, q, tile):
            hc = CHUNK_HEADS[c]
            h0 = sum(CHUNK_HEADS[:c])
            for a, m in enumerate(task_tiles(c, j)):
                nc.sync.dma_start(out=out_view[m][q][:, h0:h0 + hc, :],
                                  in_=tile[:, 128 * hc * a:128 * hc * (a + 1)].rearrange("p (h d) -> p h d", d=128))

        def content(c, j):
            oc = outs.tile([P, BANK], F32, name="oc", bufs=3)
            nc.scalar.copy(out=oc[:], in_=acc[(c, j, 0)][:])
            store(c, j, 0, oc)

        def rope_products(c, j):
            r = acc[(c, j, 1)]
            rp[(c, j)] = outs.tile([P, BANK], F32, name="rp", bufs=5)
            tm[(c, j)] = outs.tile([P, BANK], F32, name="tm", bufs=3)
            nc.vector.tensor_tensor(out=rp[(c, j)][:], in0=r[:], in1=cc4[:], op=MULT)
            nc.vector.tensor_tensor(out=tm[(c, j)][:].rearrange("p (j e) -> p j e", e=2),
                                    in0=r[:].rearrange("p (j e) -> p j e", e=2)[:, :, ::-1],
                                    in1=ss4[:].rearrange("p (j e) -> p j e", e=2), op=MULT)

        def rope_sum(c, j, eng):
            eng.tensor_tensor(out=rp[(c, j)][:], in0=rp[(c, j)][:], in1=tm[(c, j)][:], op=ADD)
            store(c, j, 1, rp[(c, j)])

        nc.scalar.dma_start(out=wsc[:], in_=s_view)
        nc.scalar.dma_start(out=cos_sb[:], in_=cos)
        nc.scalar.dma_start(out=sin_sb[:], in_=sin)
        for i in range(3):
            load_w(i)
        load_x(0)
        load_x(1)
        load_w(3)
        load_x(2)
        load_x(3)
        for i in range(4, LOADS):
            load_w(i)
        make_identity(nc, ident[:])
        make_identity(nc, ident_bf[:])

        bshape = [P, 4, 64, 2]
        nc.scalar.copy(out=cc4[:].rearrange("p (h j e) -> p h j e", h=4, e=2),
                       in_=cos_sb[:].unsqueeze(1).unsqueeze(3).to_broadcast(bshape))
        sin_b = sin_sb[:].unsqueeze(1).to_broadcast([P, 4, 64])
        ss_v = ss4[:].rearrange("p (h j e) -> p h j e", h=4, e=2)
        nc.scalar.activation(out=ss_v[:, :, :, 0], in_=sin_b, func=COPY, scale=-1.0)
        nc.scalar.copy(out=ss_v[:, :, :, 1], in_=sin_b)

        waiting = []
        filled = []
        ready = []
        summed = []

        def rope_ready():
            for task in ready:
                rope_products(task[0], task[1])
            summed.extend(ready)
            ready.clear()

        s = -LEAD - 1
        while s < UNITS or waiting or filled or ready or summed:
            widen(s + LEAD, False, (0, 1, 2))
            if 0 <= s + 1 < UNITS:
                interleave_pe(s + 1)
            if s == -1:
                x_transposes(0)
                x_transposes(1)
            done = list(filled)
            filled.clear()
            if s >= UNITS and waiting:
                for q in (1, 0):
                    for task in waiting:
                        group(task[0], task[1], q)
                filled.extend(waiting)
                waiting.clear()
            elif waiting:
                task = waiting.pop(0)
                group(task[0], task[1], 1)
                group(task[0], task[1], 0)
                filled.append(task)
            widen(s + LEAD, False, (3,))
            for task in done:
                content(task[0], task[1])
            if 0 <= s + LEAD < UNITS:
                interleave_s(s + LEAD)
            if 0 <= s < UNITS:
                interleave_v(s)
            if 0 <= s < TOK:
                x_evac(s, 0)
                x_evac(s, 1)
                if s + 2 < TOK:
                    x_transposes(s + 2)
            ready.extend(done)
            hold = UNITS - PASSES < s < UNITS
            if (ready and not hold) or (ready and not waiting and not filled and s >= UNITS):
                rope_ready()
            if 0 <= s < UNITS:
                quant(s)
                if s % PASSES == PASSES - 1:
                    c = s // PASSES
                    waiting.extend([(c, j) for j in range(CHUNK_HEADS[c])])
            if s == UNITS - 1 and ready:
                rope_ready()
            if s in (1, 3):
                x_quant(s // 2)
            widen(s + LEAD + 1, True, (0, 1, 2, 3))
            for task in summed:
                rope_sum(task[0], task[1], nc.vector)
            summed.clear()
            s += 1
